import numpy as np
import ml_dtypes


def mxq(x, axis, fmt="e4m3"):
    dtype, down = {"e4m3": (ml_dtypes.float8_e4m3fn, 7), "e5m2": (ml_dtypes.float8_e5m2, 14)}[fmt]
    v = np.moveaxis(np.asarray(x, np.float32).astype(ml_dtypes.bfloat16).astype(np.float64), axis, -1)
    blocks = v.reshape(v.shape[:-1] + (-1, 32))
    amax = np.abs(blocks).max(-1, keepdims=True)
    byte = np.maximum(np.where(amax > 0, np.frexp(amax)[1] - 1 + 127, 0) - down, 1)
    scale = np.exp2(byte - 127.0)
    codes = (blocks / scale).astype(np.float32).astype(dtype).astype(np.float64)
    return np.moveaxis((codes * scale).reshape(v.shape), -1, axis)


WIDE = False


def mx_kscale(k):
    if not WIDE:
        return np.ones(k)
    levels = np.array([10, -10, 5, -5, 0])
    if k % 512:
        return np.exp2(np.random.permutation(np.resize(levels, k // 32))).repeat(32)
    a = np.empty((k // 512, 16))
    for p in range(k // 512):
        a[p, :8] = np.random.permutation(np.resize(levels, 8))
        for g in range(8):
            far = levels[np.abs(levels - a[p, g]) >= 10]
            a[p, g + 8] = far[np.random.randint(len(far))]
    return np.exp2(a.ravel()).repeat(32)


BF16 = ml_dtypes.bfloat16


def bf(x):
    return np.asarray(x, np.float32).astype(BF16)


def f64(x):
    return np.asarray(x).astype(np.float64)


B, Nb1, Nw1, Nb2x, Nb2y, Nw2x, Nw2y, R, C = 128, 4, 16, 4, 2, 16, 16, 128, 2
J1 = Nb1 * Nb1
K1 = C * Nw1 * Nw1
J3 = Nb2x * Nb2y
L1 = J3 * R
J2 = J3 * J1


def setup_inputs():
    s = mx_kscale(K1)
    sx = s.reshape(Nw1, Nw1, C)[:, None, :, :]
    x = np.random.standard_normal((B, Nb1, Nw1, Nb1, Nw1, C)) * sx
    return {"x": bf(x.reshape(B, Nb1 * Nw1 * Nb1 * Nw1, C)),
            "k1": bf(np.random.standard_normal((J1, K1, L1)) / np.sqrt(K1) / s[None, :, None]),
            "b1": bf(np.random.standard_normal((1, J1, L1)) * 0.3)}


def core(x, k1, b1):
    h = f64(x).reshape(B, Nb1, Nw1, Nb1, Nw1, C).transpose(0, 1, 3, 2, 4, 5).reshape(B, J1, K1)
    hq = mxq(h, 2, "e4m3").transpose(1, 0, 2)
    y = (hq @ mxq(f64(k1), 1, "e4m3")).transpose(1, 0, 2) + f64(b1)
    y = y.reshape(B, J1, J3, R).transpose(0, 3, 1, 2)
    return y.reshape(B, J2, R)


def e4m3fn_bytes(y):
    return np.clip(np.asarray(y, np.float64), -448.0, 448.0).astype(np.float32).astype(ml_dtypes.float8_e4m3fn).view(np.uint8)


def reference(x, k1, b1):
    out = core(x, k1, b1)
    s = np.max(np.abs(out), axis=-1, keepdims=True) / 448.0
    return out, e4m3fn_bytes(out / s)

@@ -1,0 +1,264 @@
+from contextlib import ExitStack
+
+import concourse.mybir as mybir
+from concourse.masks import make_identity
+
+F32 = mybir.dt.float32
+BF16 = mybir.dt.bfloat16
+U32 = mybir.dt.uint32
+U8 = mybir.dt.uint8
+FP8X4 = mybir.dt.float8_e4m3fn_x4
+FP8 = mybir.dt.float8_e4m3fn
+ALU = mybir.AluOpType
+ACT = mybir.ActivationFunctionType
+AX = mybir.AxisListType
+
+P = 128
+NJ = 16
+NU = 32
+UC = 512
+CVE = 352
+GC = 0
+CHUNKS = (4, 4) + (8,) * 15
+VTAIL = 2
+SR = 16
+KBUFS = 4
+
+FLOPS = 2 * 128 * 16 * 512 * 1024
+
+
+def tile_switchnet_fstar_pa_kernel(tc, x, k1, b1, out_0, out_1):
+    nc = tc.nc
+    xf = x.rearrange("b g c -> b (g c)")
+    b1f = b1.rearrange("o j l -> (o j l)")
+
+    with ExitStack() as ctx:
+        const = ctx.enter_context(tc.tile_pool(name="const", bufs=1))
+        xsp = ctx.enter_context(tc.tile_pool(name="xsp", bufs=4))
+        xwp = ctx.enter_context(tc.tile_pool(name="xwp", bufs=2))
+        rawp = ctx.enter_context(tc.tile_pool(name="rawp", bufs=KBUFS))
+        grp = ctx.enter_context(tc.tile_pool(name="grp", bufs=2))
+        cdp = ctx.enter_context(tc.tile_pool(name="cdp", bufs=4))
+        fpp = ctx.enter_context(tc.tile_pool(name="fpp", bufs=8))
+        psx = ctx.enter_context(tc.psum_pool(name="psx", bufs=2))
+        psm = ctx.enter_context(tc.psum_pool(name="psm", bufs=6))
+
+        ident = const.tile([P, P], F32, name="ident")
+        make_identity(nc, ident[:])
+        zeros = const.tile([P, 1], F32, name="zeros")
+        nc.vector.memset(zeros[:], 0.0)
+        warm = const.tile([P, 1], F32, name="warm")
+        nc.scalar.activation(out=warm[:], in_=zeros[:], func=ACT.Identity, scale=zeros[:, 0:1], bias=zeros[:, 0:1])
+
+        hc = const.tile([P, NJ * P], U32, name="hc", align_bytes=64)
+        hs = const.tile([P, NJ * P], U8, name="hs", align_bytes=64)
+        bias = const.tile([P, NJ * 1024], BF16, name="bias")
+        big = const.tile([P, P, P], F32, name="big")
+        am = const.tile([P, P], F32, name="am")
+        sm = const.tile([P, P], F32, name="sm")
+        rs = const.tile([P, P], F32, name="rs")
+
+        raws = {}
+        xss = {}
+        x2s = {}
+        xts = {}
+        xgs = {}
+        grs = {}
+        cds = {}
+        pss = {}
+        fps = {}
+
+        def load_k(j, pieces):
+            raw = rawp.tile([P, 4, 1024], BF16, name="raw")
+            raws[j] = raw
+            src = k1[j].rearrange("(p t) l -> p t l", t=4)
+            w = 1024 // pieces
+            for i in range(pieces):
+                nc.sync.dma_start(out=raw[:, :, i * w:(i + 1) * w], in_=src[:, :, i * w:(i + 1) * w])
+
+        def load_x(br):
+            xs = xsp.tile([P, 2048], BF16, name="xs")
+            xss[br] = xs
+            nc.sync.dma_start(out=xs[:], in_=xf[:, br * 2048:(br + 1) * 2048])
+
+        def load_bias(i):
+            nc.sync.dma_start(out=bias[:, i * 2048:(i + 1) * 2048],
+                              in_=b1f[i * 2048:(i + 1) * 2048].partition_broadcast(P))
+
+        def x_regroup(br):
+            x2 = xwp.tile([P, 4, 2, P], F32, name="x2")
+            x2s[br] = x2
+            words = xss[br][:].bitcast(F32).rearrange("p (wr bc q u) -> p bc u wr q", wr=16, bc=4, q=8, u=2)
+            for u in range(2):
+                nc.vector.tensor_copy(out=x2[:, :, u, :].rearrange("p bc (wr q) -> p bc wr q", q=8),
+                                      in_=words[:, :, u, :, :])
+
+        def x_transpose(br):
+            for h in range(2):
+                xt = psx.tile([P, 2, 2, P], F32, name="xt")
+                xts[(br, h)] = xt
+                for c in range(2):
+                    for u in range(2):
+                        nc.tensor.transpose(xt[:, c, u, :], x2s[br][:, 2 * h + c, u, :], ident[:])
+
+        def x_out(br):
+            xg = xwp.tile([P, 4, P, 4], BF16, name="xg", align_bytes=64)
+            xgs[br] = xg
+            gw = xg[:].rearrange("p c b t -> p (c b t)").bitcast(F32).rearrange("p (c b u) -> p c b u", c=4, u=2)
+            for h in range(2):
+                nc.scalar.copy(out=gw[:, 2 * h:2 * h + 2, :, :], in_=xts[(br, h)][:].rearrange("p c u b -> p c b u"))
+
+        def x_quant(br):
+            sl = slice(br * 512, (br + 1) * 512)
+            nc.vector.quantize_mx(out=hc[:, sl].bitcast(FP8X4), scales=hs[:, sl],
+                                  in_=xgs[br][:].rearrange("p c b t -> p (c b t)"))
+
+        def weave(eng_copy, g, raw, a, b):
+            eng_copy(out=g[:, a:b, :].rearrange("p (c i) t -> p c t i", i=4),
+                     in_=raw[:, :, a:b].rearrange("p t (c i) -> p c t i", i=4))
+
+        def inter_alloc(j):
+            g = grp.tile([P, 1024, 4], BF16, name="g", align_bytes=64)
+            grs[j] = g
+            if GC > 0:
+                nc.gpsimd.tensor_scalar(out=g[:, 1024 - GC:1024, :],
+                                        in0=raws[j][:, :, 1024 - GC:1024].rearrange("p t c -> p c t"),
+                                        scalar1=1.0, scalar2=0.0, op0=ALU.mult, op1=ALU.add)
+
+        def inter_v(j):
+            weave(nc.vector.tensor_copy, grs[j], raws[j], 0, CVE)
+
+        def inter_s(j):
+            weave(nc.scalar.copy, grs[j], raws[j], CVE, UC)
+            weave(nc.scalar.copy, grs[j], raws[j], UC, 1024 - GC)
+
+        def quant(u):
+            kc = cdp.tile([P, UC], U32, name="kc", align_bytes=64)
+            ks = cdp.tile([P, UC], U8, name="ks", align_bytes=64)
+            cds[u] = (kc, ks)
+            c0 = (u % 2) * UC
+            nc.vector.quantize_mx(out=kc[:].bitcast(FP8X4), scales=ks[:],
+                                  in_=grs[u // 2][:, c0:c0 + UC, :].rearrange("p c t -> p (c t)"))
+
+        def mm(u):
+            j = u // 2
+            kc, ks = cds[u]
+            ps = psm.tile([P, UC], F32, name="ps")
+            pss[u] = ps
+            sl = slice(j * P, (j + 1) * P)
+            nc.tensor.matmul_mx(out=ps[:], lhsT=hc[:, sl].bitcast(FP8X4), lhsT_scale=hs[:, sl],
+                                rhs=kc[:].bitcast(FP8X4), rhs_scale=ks[:], start=True, stop=True)
+
+        def evac(u):
+            nc.vector.tensor_tensor(out=big[:, :, u * 4:(u + 1) * 4],
+                                    in0=pss[u][:].rearrange("p (m r) -> p r m", m=4),
+                                    in1=bias[:, u * UC:(u + 1) * UC].rearrange("p (m r) -> p r m", m=4),
+                                    op=ALU.add)
+
+        nch = len(CHUNKS)
+        starts = [sum(CHUNKS[:c]) for c in range(nch)]
+
+        def red(c):
+            sl = slice(starts[c], starts[c] + CHUNKS[c])
+            nc.vector.tensor_reduce(out=am[:, sl], in_=big[:, sl, :], axis=AX.X, op=ALU.max,
+                                    apply_absolute_value=True)
+            nc.gpsimd.tensor_scalar(out=sm[:, sl], in0=am[:, sl], scalar1=1.0 / 448.0, scalar2=0.0,
+                                    op0=ALU.mult, op1=ALU.add)
+
+        def factor(c):
+            sl = slice(starts[c], starts[c] + CHUNKS[c])
+            nc.vector.reciprocal(out=rs[:, sl], in_=sm[:, sl])
+
+        def casts(c):
+            for i in range(CHUNKS[c]):
+                r = starts[c] + i
+                if r % SR == 0:
+                    fps[r // SR] = fpp.tile([P, SR * P], FP8, name="fp")
+                fp = fps[r // SR]
+                dst = fp[:, (r % SR) * P:(r % SR + 1) * P]
+                if c >= nch - VTAIL and i % 2 == 0:
+                    nc.vector.tensor_scalar(out=dst, in0=big[:, r, :], scalar1=rs[:, r:r + 1], scalar2=None,
+                                            op0=ALU.mult, saturate=False)
+                else:
+                    nc.scalar.activation(out=dst, in_=big[:, r, :], func=ACT.Identity, scale=rs[:, r:r + 1],
+                                         bias=zeros[:, 0:1], saturate=False)
+
+        def store0(q):
+            nc.sync.dma_start(out=out_0[:, q * 32:(q + 1) * 32, :], in_=big[:, q * 32:(q + 1) * 32, :])
+
+        def store1(q):
+            nc.sync.dma_start(out=out_1[:, q * SR:(q + 1) * SR, :].rearrange("b r e -> b (r e)"),
+                              in_=fps[q][:].bitcast(U8))
+
+        with tc.manual_schedule():
+            load_k(0, 2)
+            for br in range(4):
+                load_x(br)
+            load_k(1, 1)
+            load_bias(0)
+            load_k(2, 1)
+            load_k(3, 1)
+            load_bias(1)
+
+            inter_alloc(0)
+            inter_v(0)
+            inter_s(0)
+            quant(0)
+            x_regroup(0)
+            x_regroup(1)
+            x_transpose(0)
+            x_out(0)
+            quant(1)
+            x_regroup(2)
+            x_transpose(1)
+            x_out(1)
+            x_quant(0)
+            x_regroup(3)
+            x_transpose(2)
+            x_out(2)
+            x_quant(1)
+            x_transpose(3)
+            x_out(3)
+            load_k(4, 1)
+            inter_alloc(1)
+            inter_v(1)
+            inter_s(1)
+            load_k(5, 1)
+            x_quant(2)
+            x_quant(3)
+            mm(0)
+            mm(1)
+            for j in range(1, NJ + 2):
+                if 1 < j <= NJ:
+                    quant(2 * j - 2)
+                    mm(2 * j - 2)
+                    quant(2 * j - 1)
+                    mm(2 * j - 1)
+                if j + 1 < NJ:
+                    inter_alloc(j + 1)
+                if j >= 2:
+                    evac(2 * j - 4)
+                    evac(2 * j - 3)
+                if j + 1 < NJ:
+                    inter_v(j + 1)
+                    inter_s(j + 1)
+                    if j + 1 + KBUFS < NJ:
+                        load_k(j + 1 + KBUFS, 1)
+                    if j % 2 == 1 and j // 2 + 2 < 8:
+                        load_bias(j // 2 + 2)
+
+            store0(0)
+            store0(1)
+            order0 = {1: 2, 3: 3}
+            red(0)
+            for c in range(nch):
+                if c + 1 < nch:
+                    red(c + 1)
+                factor(c)
+                casts(c)
+                done = starts[c] + CHUNKS[c]
+                if done % SR == 0:
+                    q = done // SR - 1
+                    store1(q)
+                    if q in order0:
+                        store0(order0[q])

@@ -17,12 +17,13 @@ P = 128
 NJ = 16
 NU = 32
 UC = 512
-CVE = 352
+CVE = 304
 GC = 0
 CHUNKS = (4, 4) + (8,) * 15
 VTAIL = 2
 SR = 16
 KBUFS = 4
+PC = 96
 
 FLOPS = 2 * 128 * 16 * 512 * 1024
 
@@ -45,6 +46,8 @@ def tile_switchnet_fstar_pa_kernel(tc, x, k1, b1, out_0, out_1):
 
         ident = const.tile([P, P], F32, name="ident")
         make_identity(nc, ident[:])
+        identb = const.tile([P, P], BF16, name="identb")
+        make_identity(nc, identb[:])
         zeros = const.tile([P, 1], F32, name="zeros")
         nc.vector.memset(zeros[:], 0.0)
         warm = const.tile([P, 1], F32, name="warm")
@@ -129,8 +132,12 @@ def tile_switchnet_fstar_pa_kernel(tc, x, k1, b1, out_0, out_1):
             weave(nc.vector.tensor_copy, grs[j], raws[j], 0, CVE)
 
         def inter_s(j):
+            pt = psx.tile([P, PC, 4], BF16, name="xt")
+            nc.tensor.matmul(out=pt[:], lhsT=identb[:], rhs=raws[j][:, :, 1024 - PC:1024].rearrange("p t c -> p c t"),
+                             start=True, stop=True)
             weave(nc.scalar.copy, grs[j], raws[j], CVE, UC)
-            weave(nc.scalar.copy, grs[j], raws[j], UC, 1024 - GC)
+            weave(nc.scalar.copy, grs[j], raws[j], UC, 1024 - PC)
+            nc.scalar.copy(out=grs[j][:, 1024 - PC:1024, :].rearrange("p c t -> p (c t)"), in_=pt[:].rearrange("p c t -> p (c t)"))
 
         def quant(u):
             kc = cdp.tile([P, UC], U32, name="kc", align_bytes=64)

@@ -23,6 +23,7 @@ CHUNKS = (4, 4) + (8,) * 15
 VTAIL = 2
 SR = 16
 KBUFS = 4
+NPB = 6
 PC = 96
 
 FLOPS = 2 * 128 * 16 * 512 * 1024
@@ -61,7 +62,11 @@ def tile_switchnet_fstar_pa_kernel(tc, x, k1, b1, out_0, out_1):
         sm = const.tile([P, P], F32, name="sm")
         rs = const.tile([P, P], F32, name="rs")
 
+        bnat = const.tile([P, P], BF16, name="bnat")
+        bt = const.tile([P, P], BF16, name="bt")
+
         raws = {}
+        pbs = {}
         xss = {}
         x2s = {}
         xts = {}
@@ -87,6 +92,24 @@ def tile_switchnet_fstar_pa_kernel(tc, x, k1, b1, out_0, out_1):
         def load_bias(i):
             nc.sync.dma_start(out=bias[:, i * 2048:(i + 1) * 2048],
                               in_=b1f[i * 2048:(i + 1) * 2048].partition_broadcast(P))
+
+        def load_bnat():
+            nc.sync.dma_start(out=bnat[:], in_=b1.rearrange("o j (m r) -> (o j m) r", r=P))
+
+        def bias_turn():
+            tp = psm.tile([P, P], BF16, name="ps")
+            nc.tensor.transpose(tp[:], bnat[:], identb[:])
+            nc.vector.tensor_copy(out=bt[:], in_=tp[:])
+
+        def bias_t(j):
+            pb = psm.tile([P, 8, P], BF16, name="ps")
+            pbs[j] = pb
+            for m in range(8):
+                nc.tensor.transpose(pb[:, m, :], bt[:, 8 * j + m:8 * j + m + 1].to_broadcast([P, P]), identb[:])
+
+        def bias_c(j):
+            eng_copy = nc.vector.tensor_copy if j % 2 == 0 else nc.scalar.copy
+            eng_copy(out=bias[:, j * 1024:(j + 1) * 1024], in_=pbs[j][:].rearrange("p m r -> p (m r)"))
 
         def x_regroup(br):
             x2 = xwp.tile([P, 4, 2, P], F32, name="x2")
@@ -198,23 +221,27 @@ def tile_switchnet_fstar_pa_kernel(tc, x, k1, b1, out_0, out_1):
                               in_=fps[q][:].bitcast(U8))
 
         with tc.manual_schedule():
+            load_bnat()
             load_k(0, 2)
             for br in range(4):
                 load_x(br)
             load_k(1, 1)
-            load_bias(0)
             load_k(2, 1)
             load_k(3, 1)
-            load_bias(1)
 
+            bias_turn()
+            bias_t(0)
+            bias_t(1)
             inter_alloc(0)
             inter_v(0)
             inter_s(0)
             quant(0)
             x_regroup(0)
             x_regroup(1)
+            bias_c(0)
             x_transpose(0)
             x_out(0)
+            bias_c(1)
             quant(1)
             x_regroup(2)
             x_transpose(1)
@@ -251,8 +278,11 @@ def tile_switchnet_fstar_pa_kernel(tc, x, k1, b1, out_0, out_1):
                     inter_s(j + 1)
                     if j + 1 + KBUFS < NJ:
                         load_k(j + 1 + KBUFS, 1)
-                    if j % 2 == 1 and j // 2 + 2 < 8:
+                    if j % 2 == 1 and NPB // 2 <= j // 2 + 2 < 8:
                         load_bias(j // 2 + 2)
+                    if j + 1 < NPB:
+                        bias_t(j + 1)
+                        bias_c(j + 1)
 
             store0(0)
             store0(1)

@@ -162,6 +162,19 @@ def tile_switchnet_fstar_pa_kernel(tc, x, k1, b1, out_0, out_1):
             weave(nc.scalar.copy, grs[j], raws[j], UC, 1024 - PC)
             nc.scalar.copy(out=grs[j][:, 1024 - PC:1024, :].rearrange("p c t -> p (c t)"), in_=pt[:].rearrange("p c t -> p (c t)"))
 
+        def inter_first():
+            g, raw = grs[0], raws[0]
+            pt = psx.tile([P, PC, 4], BF16, name="xt")
+            weave(nc.vector.tensor_copy, g, raw, 0, 176)
+            weave(nc.scalar.copy, g, raw, 176, 256)
+            weave(nc.vector.tensor_copy, g, raw, 256, 384)
+            weave(nc.scalar.copy, g, raw, 384, 512)
+            weave(nc.scalar.copy, g, raw, 512, 768)
+            nc.tensor.matmul(out=pt[:], lhsT=identb[:], rhs=raw[:, :, 1024 - PC:1024].rearrange("p t c -> p c t"),
+                             start=True, stop=True)
+            weave(nc.scalar.copy, g, raw, 768, 1024 - PC)
+            nc.scalar.copy(out=g[:, 1024 - PC:1024, :].rearrange("p c t -> p (c t)"), in_=pt[:].rearrange("p c t -> p (c t)"))
+
         def quant(u):
             kc = cdp.tile([P, UC], U32, name="kc", align_bytes=64)
             ks = cdp.tile([P, UC], U8, name="ks", align_bytes=64)
@@ -220,9 +233,15 @@ def tile_switchnet_fstar_pa_kernel(tc, x, k1, b1, out_0, out_1):
             nc.sync.dma_start(out=out_1[:, q * SR:(q + 1) * SR, :].rearrange("b r e -> b (r e)"),
                               in_=fps[q][:].bitcast(U8))
 
+        def store1_half(q, h):
+            r0 = q * SR + h * (SR // 2)
+            w = (SR // 2) * P
+            nc.sync.dma_start(out=out_1[:, r0:r0 + SR // 2, :].rearrange("b r e -> b (r e)"),
+                              in_=fps[q][:, h * w:(h + 1) * w].bitcast(U8))
+
         with tc.manual_schedule():
             load_bnat()
-            load_k(0, 2)
+            load_k(0, 4)
             for br in range(4):
                 load_x(br)
             load_k(1, 1)
@@ -233,8 +252,7 @@ def tile_switchnet_fstar_pa_kernel(tc, x, k1, b1, out_0, out_1):
             bias_t(0)
             bias_t(1)
             inter_alloc(0)
-            inter_v(0)
-            inter_s(0)
+            inter_first()
             quant(0)
             x_regroup(0)
             x_regroup(1)
@@ -294,7 +312,11 @@ def tile_switchnet_fstar_pa_kernel(tc, x, k1, b1, out_0, out_1):
                 factor(c)
                 casts(c)
                 done = starts[c] + CHUNKS[c]
-                if done % SR == 0:
+                if done == P - SR // 2:
+                    store1_half(P // SR - 1, 0)
+                elif done == P:
+                    store1_half(P // SR - 1, 1)
+                elif done % SR == 0:
                     q = done // SR - 1
                     store1(q)
                     if q in order0:

from contextlib import ExitStack

import concourse.mybir as mybir
from concourse.masks import make_identity

F32 = mybir.dt.float32
BF16 = mybir.dt.bfloat16
U32 = mybir.dt.uint32
U8 = mybir.dt.uint8
FP8X4 = mybir.dt.float8_e4m3fn_x4
FP8 = mybir.dt.float8_e4m3fn
ALU = mybir.AluOpType
ACT = mybir.ActivationFunctionType
AX = mybir.AxisListType

P = 128
NJ = 16
NU = 32
UC = 512
CVE = 304
GC = 0
CHUNKS = (4, 4) + (8,) * 15
VTAIL = 2
SR = 16
KBUFS = 4
NPB = 6
PC = 96

FLOPS = 2 * 128 * 16 * 512 * 1024


def tile_switchnet_fstar_pa_kernel(tc, x, k1, b1, out_0, out_1):
    nc = tc.nc
    xf = x.rearrange("b g c -> b (g c)")
    b1f = b1.rearrange("o j l -> (o j l)")

    with ExitStack() as ctx:
        const = ctx.enter_context(tc.tile_pool(name="const", bufs=1))
        xsp = ctx.enter_context(tc.tile_pool(name="xsp", bufs=4))
        xwp = ctx.enter_context(tc.tile_pool(name="xwp", bufs=2))
        rawp = ctx.enter_context(tc.tile_pool(name="rawp", bufs=KBUFS))
        grp = ctx.enter_context(tc.tile_pool(name="grp", bufs=2))
        cdp = ctx.enter_context(tc.tile_pool(name="cdp", bufs=4))
        fpp = ctx.enter_context(tc.tile_pool(name="fpp", bufs=8))
        psx = ctx.enter_context(tc.psum_pool(name="psx", bufs=2))
        psm = ctx.enter_context(tc.psum_pool(name="psm", bufs=6))

        ident = const.tile([P, P], F32, name="ident")
        make_identity(nc, ident[:])
        identb = const.tile([P, P], BF16, name="identb")
        make_identity(nc, identb[:])
        zeros = const.tile([P, 1], F32, name="zeros")
        nc.vector.memset(zeros[:], 0.0)
        warm = const.tile([P, 1], F32, name="warm")
        nc.scalar.activation(out=warm[:], in_=zeros[:], func=ACT.Identity, scale=zeros[:, 0:1], bias=zeros[:, 0:1])

        hc = const.tile([P, NJ * P], U32, name="hc", align_bytes=64)
        hs = const.tile([P, NJ * P], U8, name="hs", align_bytes=64)
        bias = const.tile([P, NJ * 1024], BF16, name="bias")
        big = const.tile([P, P, P], F32, name="big")
        am = const.tile([P, P], F32, name="am")
        sm = const.tile([P, P], F32, name="sm")
        rs = const.tile([P, P], F32, name="rs")

        bnat = const.tile([P, P], BF16, name="bnat")
        bt = const.tile([P, P], BF16, name="bt")

        raws = {}
        pbs = {}
        xss = {}
        x2s = {}
        xts = {}
        xgs = {}
        grs = {}
        cds = {}
        pss = {}
        fps = {}

        def load_k(j, pieces):
            raw = rawp.tile([P, 4, 1024], BF16, name="raw")
            raws[j] = raw
            src = k1[j].rearrange("(p t) l -> p t l", t=4)
            w = 1024 // pieces
            for i in range(pieces):
                nc.sync.dma_start(out=raw[:, :, i * w:(i + 1) * w], in_=src[:, :, i * w:(i + 1) * w])

        def load_x(br):
            xs = xsp.tile([P, 2048], BF16, name="xs")
            xss[br] = xs
            nc.sync.dma_start(out=xs[:], in_=xf[:, br * 2048:(br + 1) * 2048])

        def load_bias(i):
            nc.sync.dma_start(out=bias[:, i * 2048:(i + 1) * 2048],
                              in_=b1f[i * 2048:(i + 1) * 2048].partition_broadcast(P))

        def load_bnat():
            nc.sync.dma_start(out=bnat[:], in_=b1.rearrange("o j (m r) -> (o j m) r", r=P))

        def bias_turn():
            tp = psm.tile([P, P], BF16, name="ps")
            nc.tensor.transpose(tp[:], bnat[:], identb[:])
            nc.vector.tensor_copy(out=bt[:], in_=tp[:])

        def bias_t(j):
            pb = psm.tile([P, 8, P], BF16, name="ps")
            pbs[j] = pb
            for m in range(8):
                nc.tensor.transpose(pb[:, m, :], bt[:, 8 * j + m:8 * j + m + 1].to_broadcast([P, P]), identb[:])

        def bias_c(j):
            eng_copy = nc.vector.tensor_copy if j % 2 == 0 else nc.scalar.copy
            eng_copy(out=bias[:, j * 1024:(j + 1) * 1024], in_=pbs[j][:].rearrange("p m r -> p (m r)"))

        def x_regroup(br):
            x2 = xwp.tile([P, 4, 2, P], F32, name="x2")
            x2s[br] = x2
            words = xss[br][:].bitcast(F32).rearrange("p (wr bc q u) -> p bc u wr q", wr=16, bc=4, q=8, u=2)
            for u in range(2):
                nc.vector.tensor_copy(out=x2[:, :, u, :].rearrange("p bc (wr q) -> p bc wr q", q=8),
                                      in_=words[:, :, u, :, :])

        def x_transpose(br):
            for h in range(2):
                xt = psx.tile([P, 2, 2, P], F32, name="xt")
                xts[(br, h)] = xt
                for c in range(2):
                    for u in range(2):
                        nc.tensor.transpose(xt[:, c, u, :], x2s[br][:, 2 * h + c, u, :], ident[:])

        def x_out(br):
            xg = xwp.tile([P, 4, P, 4], BF16, name="xg", align_bytes=64)
            xgs[br] = xg
            gw = xg[:].rearrange("p c b t -> p (c b t)").bitcast(F32).rearrange("p (c b u) -> p c b u", c=4, u=2)
            for h in range(2):
                nc.scalar.copy(out=gw[:, 2 * h:2 * h + 2, :, :], in_=xts[(br, h)][:].rearrange("p c u b -> p c b u"))

        def x_quant(br):
            sl = slice(br * 512, (br + 1) * 512)
            nc.vector.quantize_mx(out=hc[:, sl].bitcast(FP8X4), scales=hs[:, sl],
                                  in_=xgs[br][:].rearrange("p c b t -> p (c b t)"))

        def weave(eng_copy, g, raw, a, b):
            eng_copy(out=g[:, a:b, :].rearrange("p (c i) t -> p c t i", i=4),
                     in_=raw[:, :, a:b].rearrange("p t (c i) -> p c t i", i=4))

        def inter_alloc(j):
            g = grp.tile([P, 1024, 4], BF16, name="g", align_bytes=64)
            grs[j] = g
            if GC > 0:
                nc.gpsimd.tensor_scalar(out=g[:, 1024 - GC:1024, :],
                                        in0=raws[j][:, :, 1024 - GC:1024].rearrange("p t c -> p c t"),
                                        scalar1=1.0, scalar2=0.0, op0=ALU.mult, op1=ALU.add)

        def inter_v(j):
            weave(nc.vector.tensor_copy, grs[j], raws[j], 0, CVE)

        def inter_s(j):
            pt = psx.tile([P, PC, 4], BF16, name="xt")
            nc.tensor.matmul(out=pt[:], lhsT=identb[:], rhs=raws[j][:, :, 1024 - PC:1024].rearrange("p t c -> p c t"),
                             start=True, stop=True)
            weave(nc.scalar.copy, grs[j], raws[j], CVE, UC)
            weave(nc.scalar.copy, grs[j], raws[j], UC, 1024 - PC)
            nc.scalar.copy(out=grs[j][:, 1024 - PC:1024, :].rearrange("p c t -> p (c t)"), in_=pt[:].rearrange("p c t -> p (c t)"))

        def inter_first():
            g, raw = grs[0], raws[0]
            pt = psx.tile([P, PC, 4], BF16, name="xt")
            weave(nc.vector.tensor_copy, g, raw, 0, 176)
            weave(nc.scalar.copy, g, raw, 176, 256)
            weave(nc.vector.tensor_copy, g, raw, 256, 384)
            weave(nc.scalar.copy, g, raw, 384, 512)
            weave(nc.scalar.copy, g, raw, 512, 768)
            nc.tensor.matmul(out=pt[:], lhsT=identb[:], rhs=raw[:, :, 1024 - PC:1024].rearrange("p t c -> p c t"),
                             start=True, stop=True)
            weave(nc.scalar.copy, g, raw, 768, 1024 - PC)
            nc.scalar.copy(out=g[:, 1024 - PC:1024, :].rearrange("p c t -> p (c t)"), in_=pt[:].rearrange("p c t -> p (c t)"))

        def quant(u):
            kc = cdp.tile([P, UC], U32, name="kc", align_bytes=64)
            ks = cdp.tile([P, UC], U8, name="ks", align_bytes=64)
            cds[u] = (kc, ks)
            c0 = (u % 2) * UC
            nc.vector.quantize_mx(out=kc[:].bitcast(FP8X4), scales=ks[:],
                                  in_=grs[u // 2][:, c0:c0 + UC, :].rearrange("p c t -> p (c t)"))

        def mm(u):
            j = u // 2
            kc, ks = cds[u]
            ps = psm.tile([P, UC], F32, name="ps")
            pss[u] = ps
            sl = slice(j * P, (j + 1) * P)
            nc.tensor.matmul_mx(out=ps[:], lhsT=hc[:, sl].bitcast(FP8X4), lhsT_scale=hs[:, sl],
                                rhs=kc[:].bitcast(FP8X4), rhs_scale=ks[:], start=True, stop=True)

        def evac(u):
            nc.vector.tensor_tensor(out=big[:, :, u * 4:(u + 1) * 4],
                                    in0=pss[u][:].rearrange("p (m r) -> p r m", m=4),
                                    in1=bias[:, u * UC:(u + 1) * UC].rearrange("p (m r) -> p r m", m=4),
                                    op=ALU.add)

        nch = len(CHUNKS)
        starts = [sum(CHUNKS[:c]) for c in range(nch)]

        def red(c):
            sl = slice(starts[c], starts[c] + CHUNKS[c])
            nc.vector.tensor_reduce(out=am[:, sl], in_=big[:, sl, :], axis=AX.X, op=ALU.max,
                                    apply_absolute_value=True)
            nc.gpsimd.tensor_scalar(out=sm[:, sl], in0=am[:, sl], scalar1=1.0 / 448.0, scalar2=0.0,
                                    op0=ALU.mult, op1=ALU.add)

        def factor(c):
            sl = slice(starts[c], starts[c] + CHUNKS[c])
            nc.vector.reciprocal(out=rs[:, sl], in_=sm[:, sl])

        def casts(c):
            for i in range(CHUNKS[c]):
                r = starts[c] + i
                if r % SR == 0:
                    fps[r // SR] = fpp.tile([P, SR * P], FP8, name="fp")
                fp = fps[r // SR]
                dst = fp[:, (r % SR) * P:(r % SR + 1) * P]
                if c >= nch - VTAIL and i % 2 == 0:
                    nc.vector.tensor_scalar(out=dst, in0=big[:, r, :], scalar1=rs[:, r:r + 1], scalar2=None,
                                            op0=ALU.mult, saturate=False)
                else:
                    nc.scalar.activation(out=dst, in_=big[:, r, :], func=ACT.Identity, scale=rs[:, r:r + 1],
                                         bias=zeros[:, 0:1], saturate=False)

        def store0(q):
            nc.sync.dma_start(out=out_0[:, q * 32:(q + 1) * 32, :], in_=big[:, q * 32:(q + 1) * 32, :])

        def store1(q):
            nc.sync.dma_start(out=out_1[:, q * SR:(q + 1) * SR, :].rearrange("b r e -> b (r e)"),
                              in_=fps[q][:].bitcast(U8))

        def store1_half(q, h):
            r0 = q * SR + h * (SR // 2)
            w = (SR // 2) * P
            nc.sync.dma_start(out=out_1[:, r0:r0 + SR // 2, :].rearrange("b r e -> b (r e)"),
                              in_=fps[q][:, h * w:(h + 1) * w].bitcast(U8))

        with tc.manual_schedule():
            load_bnat()
            load_k(0, 4)
            for br in range(4):
                load_x(br)
            load_k(1, 1)
            load_k(2, 1)
            load_k(3, 1)

            bias_turn()
            bias_t(0)
            bias_t(1)
            inter_alloc(0)
            inter_first()
            quant(0)
            x_regroup(0)
            x_regroup(1)
            bias_c(0)
            x_transpose(0)
            x_out(0)
            bias_c(1)
            quant(1)
            x_regroup(2)
            x_transpose(1)
            x_out(1)
            x_quant(0)
            x_regroup(3)
            x_transpose(2)
            x_out(2)
            x_quant(1)
            x_transpose(3)
            x_out(3)
            load_k(4, 1)
            inter_alloc(1)
            inter_v(1)
            inter_s(1)
            load_k(5, 1)
            x_quant(2)
            x_quant(3)
            mm(0)
            mm(1)
            for j in range(1, NJ + 2):
                if 1 < j <= NJ:
                    quant(2 * j - 2)
                    mm(2 * j - 2)
                    quant(2 * j - 1)
                    mm(2 * j - 1)
                if j + 1 < NJ:
                    inter_alloc(j + 1)
                if j >= 2:
                    evac(2 * j - 4)
                    evac(2 * j - 3)
                if j + 1 < NJ:
                    inter_v(j + 1)
                    inter_s(j + 1)
                    if j + 1 + KBUFS < NJ:
                        load_k(j + 1 + KBUFS, 1)
                    if j % 2 == 1 and NPB // 2 <= j // 2 + 2 < 8:
                        load_bias(j // 2 + 2)
                    if j + 1 < NPB:
                        bias_t(j + 1)
                        bias_c(j + 1)

            store0(0)
            store0(1)
            order0 = {1: 2, 3: 3}
            red(0)
            for c in range(nch):
                if c + 1 < nch:
                    red(c + 1)
                factor(c)
                casts(c)
                done = starts[c] + CHUNKS[c]
                if done == P - SR // 2:
                    store1_half(P // SR - 1, 0)
                elif done == P:
                    store1_half(P // SR - 1, 1)
                elif done % SR == 0:
                    q = done // SR - 1
                    store1(q)
                    if q in order0:
                        store0(order0[q])
